import numpy as np
import ml_dtypes


def mxq(x, axis, fmt="e4m3"):
    dtype, down = {"e4m3": (ml_dtypes.float8_e4m3fn, 7), "e5m2": (ml_dtypes.float8_e5m2, 14)}[fmt]
    v = np.moveaxis(np.asarray(x, np.float32).astype(ml_dtypes.bfloat16).astype(np.float64), axis, -1)
    blocks = v.reshape(v.shape[:-1] + (-1, 32))
    amax = np.abs(blocks).max(-1, keepdims=True)
    byte = np.maximum(np.where(amax > 0, np.frexp(amax)[1] - 1 + 127, 0) - down, 1)
    scale = np.exp2(byte - 127.0)
    codes = (blocks / scale).astype(np.float32).astype(dtype).astype(np.float64)
    return np.moveaxis((codes * scale).reshape(v.shape), -1, axis)


WIDE = False


def mx_kscale(k):
    if not WIDE:
        return np.ones(k)
    levels = np.array([10, -10, 5, -5, 0])
    a = np.random.permutation(np.resize(levels, k // 512 * 4)).reshape(k // 512, 4)
    idx = np.arange(k)
    return np.exp2(a[idx // 512, idx % 128 // 32])


BF16 = ml_dtypes.bfloat16


def bf(x):
    return np.asarray(x, np.float32).astype(BF16)


def f64(x):
    return np.asarray(x).astype(np.float64)


E2M1 = np.array([0.0, 0.5, 1.0, 1.5, 2.0, 3.0, 4.0, 6.0, -0.0, -0.5, -1.0, -1.5, -2.0, -3.0, -4.0, -6.0])


def pack_weight(w, fmt):
    k, n = w.shape
    w = f64(bf(w)).reshape(k // 32, 32, n)
    amax = np.abs(w).max(1)
    if fmt == "e4m3":
        byte = np.frexp(amax)[1] - 1 + 127 - 7
    else:
        mant, ex = np.frexp(amax / 6.0)
        byte = np.where(mant > 0.5, ex, ex - 1) + 127
    byte = np.clip(np.where(amax > 0, byte, 1), 1, 254)
    scaled = (w * np.exp2(127.0 - byte)[:, None, :]).reshape(k, n).astype(np.float32)
    by_word = np.ascontiguousarray(scaled.reshape(k // 512, 128, 4, n).transpose(0, 1, 3, 2))
    if fmt == "e4m3":
        words = by_word.astype(ml_dtypes.float8_e4m3fn).view(np.uint8)
    else:
        c = by_word.astype(ml_dtypes.float4_e2m1fn).view(np.uint8) & 0xF
        words = c[..., 0::2] | (c[..., 1::2] << 4)
    return np.ascontiguousarray(words), np.ascontiguousarray(byte.astype(np.uint8).reshape(k // 512, 16, n))


def unpack_weight(words, scales, fmt):
    g, p, n, _ = words.shape
    if fmt == "e4m3":
        vals = np.ascontiguousarray(words).view(ml_dtypes.float8_e4m3fn).astype(np.float64)
    else:
        nib = np.empty((g, p, n, 4), np.uint8)
        nib[..., 0::2] = words & 0xF
        nib[..., 1::2] = words >> 4
        vals = E2M1[nib]
    vals = vals * np.repeat(np.exp2(scales.astype(np.float64) - 127.0), 8, axis=1)[..., None]
    return vals.transpose(0, 1, 3, 2).reshape(g * 512, n)

def pack4(w):
    words, scales = pack_weight(w, "e2m1")
    return words.reshape(words.shape[0], 128, -1), scales


def unpack4(words, scales):
    return unpack_weight(words.reshape(words.shape[0], 128, -1, 2), scales, "e2m1")


B, IN_F, OUT_F = 2560, 512, 512
EPS = 1e-5


def setup_inputs():
    s = mx_kscale(IN_F)
    scale = 1.0 / np.sqrt(IN_F)
    x = bf(np.random.standard_normal((B, IN_F)) * s)
    y = bf(np.random.standard_normal((B, OUT_F)))
    weight = np.random.uniform(-scale, scale, (OUT_F, IN_F)) / s[None, :]
    weight_words, weight_scales = pack4(np.ascontiguousarray(weight.T))
    return {"x": x,
            "y": y,
            "weight_words": weight_words,
            "weight_scales": weight_scales,
            "bias": bf(np.random.uniform(-0.5, 0.5, OUT_F)),
            "running_mean": bf(np.random.standard_normal(OUT_F) * 0.3),
            "running_var": bf(np.random.uniform(0.5, 1.5, OUT_F)),
            "norm_weight": bf(1.0 + 0.1 * np.random.standard_normal(OUT_F)),
            "norm_bias": bf(np.random.standard_normal(OUT_F) * 0.3)}


def reference(x, y, weight_words, weight_scales, bias, running_mean, running_var, norm_weight, norm_bias):
    linear = (mxq(f64(x), 1, "e4m3") @ unpack4(weight_words, weight_scales)) + f64(bias)
    inv_std = 1.0 / np.sqrt(f64(running_var) + EPS)
    norm = (linear - f64(running_mean)) * inv_std * f64(norm_weight) + f64(norm_bias)
    return (norm + f64(y)) * f64(y)

@@ -1,0 +1,222 @@
+from contextlib import ExitStack
+
+import concourse.mybir as mybir
+from concourse.masks import make_identity
+
+F32 = mybir.dt.float32
+BF16 = mybir.dt.bfloat16
+I32 = mybir.dt.int32
+U32 = mybir.dt.uint32
+U8 = mybir.dt.uint8
+FP8X4 = mybir.dt.float8_e4m3fn_x4
+FP4X4 = mybir.dt.float4_e2m1fn_x4
+ACT = mybir.ActivationFunctionType
+ALU = mybir.AluOpType
+
+P = 128
+B, K, N = 2560, 512, 512
+NT = B // P
+NCH = N // P
+EPS = 1e-5
+FLOPS = 2 * B * K * N
+
+GROUPS = (1, 1, 2, 4, 4, 4, 4)
+X_CHUNKS = (2, 2, 4, 4, 4, 4)
+Y_CHUNK = 4
+CLS = "a" * NT
+
+
+def tile_modelnew_kernel(
+    tc, x, y, weight_words, weight_scales, bias, running_mean, running_var, norm_weight, norm_bias, out
+):
+    nc = tc.nc
+    xv = x.rearrange("(p t) k -> p t k", t=NT)
+    yv = y.rearrange("(p t) n -> p t n", t=NT)
+    ov = out.rearrange("(p t) n -> p t n", t=NT)
+    n_groups = len(GROUPS)
+    first = [sum(GROUPS[:g]) for g in range(n_groups)]
+
+    with ExitStack() as ctx:
+        sb = ctx.enter_context(tc.tile_pool(name="sb", bufs=1))
+        ps = ctx.enter_context(tc.psum_pool(name="ps", bufs=1))
+        ctx.enter_context(tc.manual_schedule())
+
+        vt = sb.tile([P, P], BF16, name="vt")
+        nc.vector.memset(vt[:], 0.0)
+        w_pl = sb.tile([P, N], U8, name="w_pl", align_bytes=64)
+        nc.vector.memset(w_pl[:].bitcast(I32), 0)
+        one = sb.tile([P, 1], F32, name="one")
+        nc.vector.memset(one[:], 1.0)
+        for v, vec in enumerate((bias, running_mean, running_var, norm_weight, norm_bias)):
+            nc.scalar.dma_start(out=vt[NCH * v : NCH * (v + 1), :], in_=vec.rearrange("(c p) -> c p", p=P))
+        warm = sb.tile([P, 1], F32, name="warm")
+        nc.scalar.activation(out=warm[:], in_=one[:], func=ACT.Sqrt)
+
+        ident_f = sb.tile([P, P], F32, name="ident_f")
+        make_identity(nc, ident_f[:])
+        ident_b = sb.tile([P, P], BF16, name="ident_b")
+        make_identity(nc, ident_b[:])
+
+        x_of = {}
+        y_of = {}
+
+        def load_x(i):
+            t0 = sum(X_CHUNKS[:i])
+            r = X_CHUNKS[i]
+            xt_sb = sb.tile([P, r, K], BF16, name="x%d" % i)
+            nc.sync.dma_start(out=xt_sb[:], in_=xv[:, t0 : t0 + r, :])
+            for j in range(r):
+                x_of[t0 + j] = xt_sb[:, j, :]
+
+        def load_y(i):
+            t0 = Y_CHUNK * i
+            y_sb = sb.tile([P, Y_CHUNK, N], BF16, name="y%d" % i)
+            nc.sync.dma_start(out=y_sb[:], in_=yv[:, t0 : t0 + Y_CHUNK, :])
+            for j in range(Y_CHUNK):
+                y_of[t0 + j] = y_sb[:, j, :]
+
+        load_x(0)
+        w_sb = sb.tile([P, 2 * N], U8, name="w_sb", align_bytes=64)
+        nc.sync.dma_start(out=w_sb[:].bitcast(I32), in_=weight_words[0].bitcast(I32))
+        for r in range(4):
+            nc.sync.dma_start(out=w_pl[r:P:32, :].bitcast(I32), in_=weight_scales[0, r:16:4, :].bitcast(I32))
+        load_x(1)
+        load_y(0)
+        load_x(2)
+        load_x(3)
+        load_y(1)
+        load_x(4)
+        load_y(2)
+        load_x(5)
+        load_y(3)
+        load_y(4)
+
+        banks = {}
+        grouped_of = {}
+        codes_of = {}
+        plane_of = {}
+        zt_of = {}
+
+        def s1(g):
+            r = GROUPS[g]
+            tiles = []
+            for b0 in range(0, r, 2):
+                cnt = min(2, r - b0)
+                xt = ps.tile([P, 2, P * cnt], F32, name="xt%d_%d" % (g, b0), tag="xt", bufs=2)
+                for jj in range(cnt):
+                    xw = x_of[first[g] + b0 + jj].bitcast(F32)
+                    for u in range(2):
+                        nc.tensor.transpose(xt[:, u, P * jj : P * (jj + 1)], xw[:, u : K // 2 : 2], ident_f[:])
+                tiles.append((b0, cnt, xt))
+            banks[g] = tiles
+
+        def s2(g):
+            r = GROUPS[g]
+            grouped = sb.tile([P, 4 * P * r], BF16, name="grp%d" % g, align_bytes=64)
+            gv = grouped[:].bitcast(F32).rearrange("p (r u) -> p r u", u=2)
+            for b0, cnt, xt in banks[g]:
+                nc.scalar.copy(out=gv[:, P * b0 : P * (b0 + cnt), :], in_=xt[:].rearrange("p u r -> p r u"))
+            grouped_of[g] = grouped
+
+        def s3(g):
+            r = GROUPS[g]
+            codes = sb.tile([P, P * r], U32, name="codes%d" % g, align_bytes=64)
+            plane = sb.tile([P, P * r], U8, name="plane%d" % g, align_bytes=64)
+            nc.vector.quantize_mx(out=codes[:].bitcast(FP8X4), scales=plane[:], in_=grouped_of[g][:])
+            codes_of[g] = codes
+            plane_of[g] = plane
+
+        def front(g):
+            s1(g)
+            s2(g)
+            s3(g)
+
+        s1(0)
+        s2(0)
+        vps = ps.tile([P, P], BF16, name="vps", tag="xt", bufs=2)
+        nc.tensor.transpose(vps[:], vt[:], ident_b[:])
+        vv = sb.tile([P, 5 * NCH], F32, name="vv")
+        nc.vector.tensor_copy(out=vv[:], in_=vps[:, 0 : 5 * NCH])
+        c_bias = vv[:, 0:NCH]
+        c_mean = vv[:, NCH : 2 * NCH]
+        c_var = vv[:, 2 * NCH : 3 * NCH]
+        c_nw = vv[:, 3 * NCH : 4 * NCH]
+        c_nb = vv[:, 4 * NCH : 5 * NCH]
+        ve = sb.tile([P, NCH], F32, name="ve")
+        nc.vector.tensor_scalar_add(out=ve[:], in0=c_var, scalar1=EPS)
+        sd = sb.tile([P, NCH], F32, name="sd")
+        nc.scalar.activation(out=sd[:], in_=ve[:], func=ACT.Sqrt)
+        s3(0)
+        dm = sb.tile([P, NCH], F32, name="dm")
+        nc.vector.tensor_tensor(out=dm[:], in0=c_bias, in1=c_mean, op=ALU.subtract)
+        rs = sb.tile([P, NCH], F32, name="rs")
+        nc.vector.reciprocal(out=rs[:], in_=sd[:])
+        a_sc = sb.tile([P, NCH], F32, name="a_sc")
+        nc.vector.tensor_tensor(out=a_sc[:], in0=rs[:], in1=c_nw, op=ALU.mult)
+        da = sb.tile([P, NCH], F32, name="da")
+        nc.vector.tensor_tensor(out=da[:], in0=dm[:], in1=a_sc[:], op=ALU.mult)
+        c_sh = sb.tile([P, NCH], F32, name="c_sh")
+        nc.vector.tensor_tensor(out=c_sh[:], in0=da[:], in1=c_nb, op=ALU.add)
+        front(1)
+
+        def mx(g):
+            r = GROUPS[g]
+            zts = []
+            for c in range(NCH):
+                lin = ps.tile([P, P * r], F32, name="lin%d_%d" % (g, c), tag="lin", bufs=3)
+                nc.tensor.matmul_mx(
+                    out=lin[:],
+                    lhsT=w_sb[:, 2 * P * c : 2 * P * (c + 1)].bitcast(FP4X4),
+                    lhsT_scale=w_pl[:, P * c : P * (c + 1)],
+                    rhs=codes_of[g][:].bitcast(FP8X4),
+                    rhs_scale=plane_of[g][:],
+                    start=True,
+                    stop=True,
+                )
+                zt = sb.tile([P, P * r], F32, name="zt%d_%d" % (g, c))
+                nc.scalar.activation(
+                    out=zt[:], in_=lin[:], func=ACT.Identity, bias=c_sh[:, c : c + 1], scale=a_sc[:, c : c + 1]
+                )
+                zts.append(zt)
+            zt_of[g] = zts
+
+        res_of = {}
+        pending = []
+
+        def finish(t):
+            res = res_of[t]
+            if CLS[t] == "b":
+                nc.gpsimd.tensor_tensor(out=res, in0=res, in1=y_of[t], op=ALU.mult)
+            else:
+                nc.vector.tensor_tensor(out=res, in0=res, in1=y_of[t], op=ALU.mult)
+            if t >= NT - 2:
+                nc.sync.dma_start(out=ov[:, t, :], in_=res)
+            elif t % 2 == 1:
+                nc.sync.dma_start(out=ov[:, t - 1 : t + 1, :], in_=pair_of[t][:])
+
+        pair_of = {}
+
+        def back(g):
+            for j in range(GROUPS[g]):
+                t = first[g] + j
+                zb = ps.tile([P, N], F32, name="zb%d" % t, tag="zb", bufs=3)
+                for c in range(NCH):
+                    nc.tensor.transpose(zb[:, P * c : P * (c + 1)], zt_of[g][c][:, P * j : P * (j + 1)], ident_f[:])
+                if t % 2 == 0:
+                    pair = sb.tile([P, 2, N], F32, name="res%d" % t)
+                    pair_of[t] = pair
+                    pair_of[t + 1] = pair
+                res_of[t] = pair_of[t][:, t % 2, :]
+                nc.vector.tensor_tensor(out=res_of[t], in0=zb[:], in1=y_of[t], op=ALU.add)
+                if pending:
+                    finish(pending.pop())
+                pending.append(t)
+
+        for g in range(n_groups):
+            mx(g)
+            if g >= 1:
+                back(g - 1)
+            if g + 2 < n_groups:
+                front(g + 2)
+        back(n_groups - 1)
+        finish(pending.pop())

@@ -20,10 +20,13 @@ NCH = N // P
 EPS = 1e-5
 FLOPS = 2 * B * K * N
 
-GROUPS = (1, 1, 2, 4, 4, 4, 4)
-X_CHUNKS = (2, 2, 4, 4, 4, 4)
-Y_CHUNK = 4
-CLS = "a" * NT
+GROUPS = (2, 2, 4, 4, 4, 2, 2)
+LOADS = (("x", 0, 2), ("x", 2, 4), ("w", 0, 0), ("s", 0, 0), ("x", 4, 8), ("x", 8, 12), ("y", 0, 4), ("x", 12, 16), ("x", 16, 20), ("y", 4, 8), ("y", 8, 12), ("y", 12, 16), ("y", 16, 20))
+CLS = "bbbabbbabbbabbbabbaa"
+AHEAD = 2
+PRE = 1
+S2_VECTOR = ((0, 0), (1, 0), (2, 2), (3, 2), (4, 2))
+PINNED = True
 
 
 def tile_modelnew_kernel(
@@ -38,8 +41,12 @@ def tile_modelnew_kernel(
 
     with ExitStack() as ctx:
         sb = ctx.enter_context(tc.tile_pool(name="sb", bufs=1))
-        ps = ctx.enter_context(tc.psum_pool(name="ps", bufs=1))
-        ctx.enter_context(tc.manual_schedule())
+        ps = ctx.enter_context(tc.psum_pool(name="ps", bufs=8))
+        if PINNED:
+            ctx.enter_context(tc.manual_schedule())
+
+        def bank(shape, dtype, name):
+            return ps.tile(shape, dtype, name=name, tag="bank")
 
         vt = sb.tile([P, P], BF16, name="vt")
         nc.vector.memset(vt[:], 0.0)
@@ -57,65 +64,55 @@ def tile_modelnew_kernel(
         ident_b = sb.tile([P, P], BF16, name="ident_b")
         make_identity(nc, ident_b[:])
 
+        w_sb = sb.tile([P, 2 * N], U8, name="w_sb", align_bytes=64)
         x_of = {}
         y_of = {}
+        for what, t0, t1 in LOADS:
+            if what == "w":
+                nc.sync.dma_start(out=w_sb[:].bitcast(I32), in_=weight_words[0].bitcast(I32))
+            elif what == "s":
+                for r in range(4):
+                    nc.sync.dma_start(out=w_pl[r:P:32, :].bitcast(I32), in_=weight_scales[0, r:16:4, :].bitcast(I32))
+            else:
+                src, table = (xv, x_of) if what == "x" else (yv, y_of)
+                chunk = sb.tile([P, t1 - t0, K], BF16, name="%s%d" % (what, t0))
+                nc.sync.dma_start(out=chunk[:], in_=src[:, t0:t1, :])
+                for t in range(t0, t1):
+                    table[t] = chunk[:, t - t0, :]
 
-        def load_x(i):
-            t0 = sum(X_CHUNKS[:i])
-            r = X_CHUNKS[i]
-            xt_sb = sb.tile([P, r, K], BF16, name="x%d" % i)
-            nc.sync.dma_start(out=xt_sb[:], in_=xv[:, t0 : t0 + r, :])
-            for j in range(r):
-                x_of[t0 + j] = xt_sb[:, j, :]
-
-        def load_y(i):
-            t0 = Y_CHUNK * i
-            y_sb = sb.tile([P, Y_CHUNK, N], BF16, name="y%d" % i)
-            nc.sync.dma_start(out=y_sb[:], in_=yv[:, t0 : t0 + Y_CHUNK, :])
-            for j in range(Y_CHUNK):
-                y_of[t0 + j] = y_sb[:, j, :]
-
-        load_x(0)
-        w_sb = sb.tile([P, 2 * N], U8, name="w_sb", align_bytes=64)
-        nc.sync.dma_start(out=w_sb[:].bitcast(I32), in_=weight_words[0].bitcast(I32))
-        for r in range(4):
-            nc.sync.dma_start(out=w_pl[r:P:32, :].bitcast(I32), in_=weight_scales[0, r:16:4, :].bitcast(I32))
-        load_x(1)
-        load_y(0)
-        load_x(2)
-        load_x(3)
-        load_y(1)
-        load_x(4)
-        load_y(2)
-        load_x(5)
-        load_y(3)
-        load_y(4)
-
-        banks = {}
+        xt_of = {}
         grouped_of = {}
         codes_of = {}
         plane_of = {}
         zt_of = {}
+        zb_of = {}
+        res_of = {}
+        pair_of = {}
 
         def s1(g):
             r = GROUPS[g]
             tiles = []
             for b0 in range(0, r, 2):
                 cnt = min(2, r - b0)
-                xt = ps.tile([P, 2, P * cnt], F32, name="xt%d_%d" % (g, b0), tag="xt", bufs=2)
+                xt = bank([P, 2, P * cnt], F32, "xt%d_%d" % (g, b0))
                 for jj in range(cnt):
                     xw = x_of[first[g] + b0 + jj].bitcast(F32)
                     for u in range(2):
                         nc.tensor.transpose(xt[:, u, P * jj : P * (jj + 1)], xw[:, u : K // 2 : 2], ident_f[:])
                 tiles.append((b0, cnt, xt))
-            banks[g] = tiles
+            xt_of[g] = tiles
 
         def s2(g):
             r = GROUPS[g]
             grouped = sb.tile([P, 4 * P * r], BF16, name="grp%d" % g, align_bytes=64)
             gv = grouped[:].bitcast(F32).rearrange("p (r u) -> p r u", u=2)
-            for b0, cnt, xt in banks[g]:
-                nc.scalar.copy(out=gv[:, P * b0 : P * (b0 + cnt), :], in_=xt[:].rearrange("p u r -> p r u"))
+            for b0, cnt, xt in xt_of[g]:
+                dst = gv[:, P * b0 : P * (b0 + cnt), :]
+                src = xt[:].rearrange("p u r -> p r u")
+                if (g, b0) in S2_VECTOR:
+                    nc.vector.tensor_copy(out=dst, in_=src)
+                else:
+                    nc.scalar.copy(out=dst, in_=src)
             grouped_of[g] = grouped
 
         def s3(g):
@@ -126,14 +123,9 @@ def tile_modelnew_kernel(
             codes_of[g] = codes
             plane_of[g] = plane
 
-        def front(g):
-            s1(g)
-            s2(g)
-            s3(g)
-
         s1(0)
         s2(0)
-        vps = ps.tile([P, P], BF16, name="vps", tag="xt", bufs=2)
+        vps = bank([P, P], BF16, "vps")
         nc.tensor.transpose(vps[:], vt[:], ident_b[:])
         vv = sb.tile([P, 5 * NCH], F32, name="vv")
         nc.vector.tensor_copy(out=vv[:], in_=vps[:, 0 : 5 * NCH])
@@ -146,9 +138,9 @@ def tile_modelnew_kernel(
         nc.vector.tensor_scalar_add(out=ve[:], in0=c_var, scalar1=EPS)
         sd = sb.tile([P, NCH], F32, name="sd")
         nc.scalar.activation(out=sd[:], in_=ve[:], func=ACT.Sqrt)
-        s3(0)
         dm = sb.tile([P, NCH], F32, name="dm")
         nc.vector.tensor_tensor(out=dm[:], in0=c_bias, in1=c_mean, op=ALU.subtract)
+        s3(0)
         rs = sb.tile([P, NCH], F32, name="rs")
         nc.vector.reciprocal(out=rs[:], in_=sd[:])
         a_sc = sb.tile([P, NCH], F32, name="a_sc")
@@ -157,13 +149,16 @@ def tile_modelnew_kernel(
         nc.vector.tensor_tensor(out=da[:], in0=dm[:], in1=a_sc[:], op=ALU.mult)
         c_sh = sb.tile([P, NCH], F32, name="c_sh")
         nc.vector.tensor_tensor(out=c_sh[:], in0=da[:], in1=c_nb, op=ALU.add)
-        front(1)
+        for g in range(1, min(AHEAD, n_groups)):
+            s1(g)
+            s2(g)
+            s3(g)
 
         def mx(g):
             r = GROUPS[g]
             zts = []
             for c in range(NCH):
-                lin = ps.tile([P, P * r], F32, name="lin%d_%d" % (g, c), tag="lin", bufs=3)
+                lin = bank([P, P * r], F32, "lin%d_%d" % (g, c))
                 nc.tensor.matmul_mx(
                     out=lin[:],
                     lhsT=w_sb[:, 2 * P * c : 2 * P * (c + 1)].bitcast(FP4X4),
@@ -180,8 +175,20 @@ def tile_modelnew_kernel(
                 zts.append(zt)
             zt_of[g] = zts
 
-        res_of = {}
-        pending = []
+        def s6(g, t):
+            j = t - first[g]
+            zb = bank([P, N], F32, "zb%d" % t)
+            for c in range(NCH):
+                nc.tensor.transpose(zb[:, P * c : P * (c + 1)], zt_of[g][c][:, P * j : P * (j + 1)], ident_f[:])
+            zb_of[t] = zb
+
+        def p1(t):
+            if t % 2 == 0:
+                pair = sb.tile([P, 2, N], F32, name="res%d" % t)
+                pair_of[t] = pair
+                pair_of[t + 1] = pair
+            res_of[t] = pair_of[t][:, t % 2, :]
+            nc.vector.tensor_tensor(out=res_of[t], in0=zb_of[t][:], in1=y_of[t], op=ALU.add)
 
         def finish(t):
             res = res_of[t]
@@ -194,29 +201,23 @@ def tile_modelnew_kernel(
             elif t % 2 == 1:
                 nc.sync.dma_start(out=ov[:, t - 1 : t + 1, :], in_=pair_of[t][:])
 
-        pair_of = {}
-
-        def back(g):
-            for j in range(GROUPS[g]):
-                t = first[g] + j
-                zb = ps.tile([P, N], F32, name="zb%d" % t, tag="zb", bufs=3)
-                for c in range(NCH):
-                    nc.tensor.transpose(zb[:, P * c : P * (c + 1)], zt_of[g][c][:, P * j : P * (j + 1)], ident_f[:])
-                if t % 2 == 0:
-                    pair = sb.tile([P, 2, N], F32, name="res%d" % t)
-                    pair_of[t] = pair
-                    pair_of[t + 1] = pair
-                res_of[t] = pair_of[t][:, t % 2, :]
-                nc.vector.tensor_tensor(out=res_of[t], in0=zb[:], in1=y_of[t], op=ALU.add)
-                if pending:
-                    finish(pending.pop())
-                pending.append(t)
-
-        for g in range(n_groups):
-            mx(g)
-            if g >= 1:
-                back(g - 1)
-            if g + 2 < n_groups:
-                front(g + 2)
-        back(n_groups - 1)
-        finish(pending.pop())
+        for g in range(n_groups + 1):
+            if g < n_groups:
+                mx(g)
+            back = list(range(first[g - 1], first[g - 1] + GROUPS[g - 1])) if g >= 1 else []
+            ahead = g + AHEAD if g + AHEAD < n_groups else None
+            for t in back[:PRE]:
+                s6(g - 1, t)
+            if ahead is not None:
+                s1(ahead)
+            for t in back[PRE:]:
+                s6(g - 1, t)
+            if ahead is not None:
+                s2(ahead)
+            for t in back:
+                p1(t)
+                if t >= 1:
+                    finish(t - 1)
+            if ahead is not None:
+                s3(ahead)
+        finish(NT - 1)

@@ -22,10 +22,10 @@ FLOPS = 2 * B * K * N
 
 GROUPS = (2, 2, 4, 4, 4, 2, 2)
 LOADS = (("x", 0, 2), ("x", 2, 4), ("w", 0, 0), ("s", 0, 0), ("x", 4, 8), ("x", 8, 12), ("y", 0, 4), ("x", 12, 16), ("x", 16, 20), ("y", 4, 8), ("y", 8, 12), ("y", 12, 16), ("y", 16, 20))
-CLS = "bbbabbbabbbabbbabbaa"
+CLS = "abcabcabcabcabcabcac"
 AHEAD = 2
 PRE = 1
-S2_VECTOR = ((0, 0), (1, 0), (2, 2), (3, 2), (4, 2))
+S2_VECTOR = ((0, 0), (1, 0))
 PINNED = True
 
 
@@ -178,8 +178,20 @@ def tile_modelnew_kernel(
         def s6(g, t):
             j = t - first[g]
             zb = bank([P, N], F32, "zb%d" % t)
+            if CLS[t] == "c":
+                nc.tensor.matmul(out=zb[:], lhsT=ident_b[:], rhs=y_of[t], start=True, stop=False)
             for c in range(NCH):
-                nc.tensor.transpose(zb[:, P * c : P * (c + 1)], zt_of[g][c][:, P * j : P * (j + 1)], ident_f[:])
+                if CLS[t] == "c":
+                    nc.tensor.matmul(
+                        out=zb[:, P * c : P * (c + 1)],
+                        lhsT=zt_of[g][c][:, P * j : P * (j + 1)],
+                        rhs=ident_f[:],
+                        is_transpose=True,
+                        start=False,
+                        stop=(c == NCH - 1),
+                    )
+                else:
+                    nc.tensor.transpose(zb[:, P * c : P * (c + 1)], zt_of[g][c][:, P * j : P * (j + 1)], ident_f[:])
             zb_of[t] = zb
 
         def p1(t):
@@ -188,13 +200,13 @@ def tile_modelnew_kernel(
                 pair_of[t] = pair
                 pair_of[t + 1] = pair
             res_of[t] = pair_of[t][:, t % 2, :]
-            nc.vector.tensor_tensor(out=res_of[t], in0=zb_of[t][:], in1=y_of[t], op=ALU.add)
+            nc.vector.tensor_tensor(out=res_of[t], in0=zb_of[t][:], in1=y_of[t], op=ALU.mult if CLS[t] == "c" else ALU.add)
 
         def finish(t):
             res = res_of[t]
             if CLS[t] == "b":
                 nc.gpsimd.tensor_tensor(out=res, in0=res, in1=y_of[t], op=ALU.mult)
-            else:
+            elif CLS[t] == "a":
                 nc.vector.tensor_tensor(out=res, in0=res, in1=y_of[t], op=ALU.mult)
             if t >= NT - 2:
                 nc.sync.dma_start(out=ov[:, t, :], in_=res)

@@ -21,11 +21,12 @@ EPS = 1e-5
 FLOPS = 2 * B * K * N
 
 GROUPS = (2, 2, 4, 4, 4, 2, 2)
-LOADS = (("x", 0, 2), ("x", 2, 4), ("w", 0, 0), ("s", 0, 0), ("x", 4, 8), ("x", 8, 12), ("y", 0, 4), ("x", 12, 16), ("x", 16, 20), ("y", 4, 8), ("y", 8, 12), ("y", 12, 16), ("y", 16, 20))
-CLS = "abcabcabcabcabcabcac"
-AHEAD = 2
-PRE = 1
+LOADS = (("x", 0, 2), ("x", 2, 4), ("x", 4, 8), ("w", 0, 0), ("s", 0, 0), ("x", 8, 12), ("y", 0, 4), ("x", 12, 16), ("x", 16, 20), ("y", 4, 8), ("y", 8, 12), ("y", 12, 16), ("y", 16, 20))
+CLS = "abababcabcabcabcaccc"
+AHEAD = 3
+PRE = 4
 S2_VECTOR = ((0, 0), (1, 0))
+S5_VECTOR = ((0, 1), (0, 3), (1, 1), (1, 3))
 PINNED = True
 
 
@@ -123,8 +124,6 @@ def tile_modelnew_kernel(
             codes_of[g] = codes
             plane_of[g] = plane
 
-        s1(0)
-        s2(0)
         vps = bank([P, P], BF16, "vps")
         nc.tensor.transpose(vps[:], vt[:], ident_b[:])
         vv = sb.tile([P, 5 * NCH], F32, name="vv")
@@ -140,7 +139,6 @@ def tile_modelnew_kernel(
         nc.scalar.activation(out=sd[:], in_=ve[:], func=ACT.Sqrt)
         dm = sb.tile([P, NCH], F32, name="dm")
         nc.vector.tensor_tensor(out=dm[:], in0=c_bias, in1=c_mean, op=ALU.subtract)
-        s3(0)
         rs = sb.tile([P, NCH], F32, name="rs")
         nc.vector.reciprocal(out=rs[:], in_=sd[:])
         a_sc = sb.tile([P, NCH], F32, name="a_sc")
@@ -149,7 +147,7 @@ def tile_modelnew_kernel(
         nc.vector.tensor_tensor(out=da[:], in0=dm[:], in1=a_sc[:], op=ALU.mult)
         c_sh = sb.tile([P, NCH], F32, name="c_sh")
         nc.vector.tensor_tensor(out=c_sh[:], in0=da[:], in1=c_nb, op=ALU.add)
-        for g in range(1, min(AHEAD, n_groups)):
+        for g in range(min(AHEAD, n_groups)):
             s1(g)
             s2(g)
             s3(g)
@@ -169,9 +167,19 @@ def tile_modelnew_kernel(
                     stop=True,
                 )
                 zt = sb.tile([P, P * r], F32, name="zt%d_%d" % (g, c))
-                nc.scalar.activation(
-                    out=zt[:], in_=lin[:], func=ACT.Identity, bias=c_sh[:, c : c + 1], scale=a_sc[:, c : c + 1]
-                )
+                if (g, c) in S5_VECTOR:
+                    nc.vector.tensor_scalar(
+                        out=zt[:],
+                        in0=lin[:],
+                        scalar1=a_sc[:, c : c + 1],
+                        scalar2=c_sh[:, c : c + 1],
+                        op0=ALU.mult,
+                        op1=ALU.add,
+                    )
+                else:
+                    nc.scalar.activation(
+                        out=zt[:], in_=lin[:], func=ACT.Identity, bias=c_sh[:, c : c + 1], scale=a_sc[:, c : c + 1]
+                    )
                 zts.append(zt)
             zt_of[g] = zts
 

@@ -50,7 +50,7 @@ def tile_modelnew_kernel(
             return ps.tile(shape, dtype, name=name, tag="bank")
 
         vt = sb.tile([P, P], BF16, name="vt")
-        nc.vector.memset(vt[:], 0.0)
+        nc.gpsimd.memset(vt[:], 0.0)
         w_pl = sb.tile([P, N], U8, name="w_pl", align_bytes=64)
         nc.vector.memset(w_pl[:].bitcast(I32), 0)
         one = sb.tile([P, 1], F32, name="one")
@@ -124,6 +124,8 @@ def tile_modelnew_kernel(
             codes_of[g] = codes
             plane_of[g] = plane
 
+        s1(0)
+        s2(0)
         vps = bank([P, P], BF16, "vps")
         nc.tensor.transpose(vps[:], vt[:], ident_b[:])
         vv = sb.tile([P, 5 * NCH], F32, name="vv")
@@ -139,6 +141,7 @@ def tile_modelnew_kernel(
         nc.scalar.activation(out=sd[:], in_=ve[:], func=ACT.Sqrt)
         dm = sb.tile([P, NCH], F32, name="dm")
         nc.vector.tensor_tensor(out=dm[:], in0=c_bias, in1=c_mean, op=ALU.subtract)
+        s3(0)
         rs = sb.tile([P, NCH], F32, name="rs")
         nc.vector.reciprocal(out=rs[:], in_=sd[:])
         a_sc = sb.tile([P, NCH], F32, name="a_sc")
@@ -147,7 +150,7 @@ def tile_modelnew_kernel(
         nc.vector.tensor_tensor(out=da[:], in0=dm[:], in1=a_sc[:], op=ALU.mult)
         c_sh = sb.tile([P, NCH], F32, name="c_sh")
         nc.vector.tensor_tensor(out=c_sh[:], in0=da[:], in1=c_nb, op=ALU.add)
-        for g in range(min(AHEAD, n_groups)):
+        for g in range(1, min(AHEAD, n_groups)):
             s1(g)
             s2(g)
             s3(g)

@@ -22,10 +22,10 @@ FLOPS = 2 * B * K * N
 
 GROUPS = (2, 2, 4, 4, 4, 2, 2)
 LOADS = (("x", 0, 2), ("x", 2, 4), ("x", 4, 8), ("w", 0, 0), ("s", 0, 0), ("x", 8, 12), ("y", 0, 4), ("x", 12, 16), ("x", 16, 20), ("y", 4, 8), ("y", 8, 12), ("y", 12, 16), ("y", 16, 20))
-CLS = "abababcabcabcabcaccc"
+CLS = "abababcbbcabccbcacca"
 AHEAD = 3
 PRE = 4
-S2_VECTOR = ((0, 0), (1, 0))
+S2_VECTOR = ((0, 0), (2, 0), (2, 2))
 S5_VECTOR = ((0, 1), (0, 3), (1, 1), (1, 3))
 PINNED = True
 

@@ -22,10 +22,10 @@ FLOPS = 2 * B * K * N
 
 GROUPS = (2, 2, 4, 4, 4, 2, 2)
 LOADS = (("x", 0, 2), ("x", 2, 4), ("x", 4, 8), ("w", 0, 0), ("s", 0, 0), ("x", 8, 12), ("y", 0, 4), ("x", 12, 16), ("x", 16, 20), ("y", 4, 8), ("y", 8, 12), ("y", 12, 16), ("y", 16, 20))
-CLS = "abababcbbcabccbcacca"
+CLS = "abababcabcabcabcaccc"
 AHEAD = 3
 PRE = 4
-S2_VECTOR = ((0, 0), (2, 0), (2, 2))
+S2_VECTOR = ((0, 0), (1, 0))
 S5_VECTOR = ((0, 1), (0, 3), (1, 1), (1, 3))
 PINNED = True
 
@@ -188,9 +188,10 @@ def tile_modelnew_kernel(
 
         def s6(g, t):
             j = t - first[g]
-            zb = bank([P, N], F32, "zb%d" % t)
             if CLS[t] == "c":
-                nc.tensor.matmul(out=zb[:], lhsT=ident_b[:], rhs=y_of[t], start=True, stop=False)
+                zb = zb_of[t]
+            else:
+                zb = bank([P, N], F32, "zb%d" % t)
             for c in range(NCH):
                 if CLS[t] == "c":
                     nc.tensor.matmul(
@@ -203,6 +204,11 @@ def tile_modelnew_kernel(
                     )
                 else:
                     nc.tensor.transpose(zb[:, P * c : P * (c + 1)], zt_of[g][c][:, P * j : P * (j + 1)], ident_f[:])
+            zb_of[t] = zb
+
+        def add_y(t):
+            zb = bank([P, N], F32, "zb%d" % t)
+            nc.tensor.matmul(out=zb[:], lhsT=ident_b[:], rhs=y_of[t], start=True, stop=False)
             zb_of[t] = zb
 
         def p1(t):
@@ -229,6 +235,9 @@ def tile_modelnew_kernel(
                 mx(g)
             back = list(range(first[g - 1], first[g - 1] + GROUPS[g - 1])) if g >= 1 else []
             ahead = g + AHEAD if g + AHEAD < n_groups else None
+            for t in back:
+                if CLS[t] == "c":
+                    add_y(t)
             for t in back[:PRE]:
                 s6(g - 1, t)
             if ahead is not None:

@@ -235,14 +235,15 @@ def tile_modelnew_kernel(
                 mx(g)
             back = list(range(first[g - 1], first[g - 1] + GROUPS[g - 1])) if g >= 1 else []
             ahead = g + AHEAD if g + AHEAD < n_groups else None
-            for t in back:
+            for t in back[:PRE]:
                 if CLS[t] == "c":
                     add_y(t)
-            for t in back[:PRE]:
                 s6(g - 1, t)
             if ahead is not None:
                 s1(ahead)
             for t in back[PRE:]:
+                if CLS[t] == "c":
+                    add_y(t)
                 s6(g - 1, t)
             if ahead is not None:
                 s2(ahead)

@@ -21,7 +21,7 @@ EPS = 1e-5
 FLOPS = 2 * B * K * N
 
 GROUPS = (2, 2, 4, 4, 4, 2, 2)
-LOADS = (("x", 0, 2), ("x", 2, 4), ("x", 4, 8), ("w", 0, 0), ("s", 0, 0), ("x", 8, 12), ("y", 0, 4), ("x", 12, 16), ("x", 16, 20), ("y", 4, 8), ("y", 8, 12), ("y", 12, 16), ("y", 16, 20))
+LOADS = (("x", 0, 2), ("v", 0, 0), ("x", 2, 4), ("x", 4, 8), ("w", 0, 0), ("s", 0, 0), ("x", 8, 12), ("y", 0, 4), ("x", 12, 16), ("x", 16, 20), ("y", 4, 8), ("y", 8, 12), ("y", 12, 16), ("y", 16, 20))
 CLS = "abababcabcabcabcaccc"
 AHEAD = 3
 PRE = 4
@@ -55,8 +55,6 @@ def tile_modelnew_kernel(
         nc.vector.memset(w_pl[:].bitcast(I32), 0)
         one = sb.tile([P, 1], F32, name="one")
         nc.vector.memset(one[:], 1.0)
-        for v, vec in enumerate((bias, running_mean, running_var, norm_weight, norm_bias)):
-            nc.scalar.dma_start(out=vt[NCH * v : NCH * (v + 1), :], in_=vec.rearrange("(c p) -> c p", p=P))
         warm = sb.tile([P, 1], F32, name="warm")
         nc.scalar.activation(out=warm[:], in_=one[:], func=ACT.Sqrt)
 
@@ -69,7 +67,10 @@ def tile_modelnew_kernel(
         x_of = {}
         y_of = {}
         for what, t0, t1 in LOADS:
-            if what == "w":
+            if what == "v":
+                for v, vec in enumerate((bias, running_mean, running_var, norm_weight, norm_bias)):
+                    nc.sync.dma_start(out=vt[NCH * v : NCH * (v + 1), :], in_=vec.rearrange("(c p) -> c p", p=P))
+            elif what == "w":
                 nc.sync.dma_start(out=w_sb[:].bitcast(I32), in_=weight_words[0].bitcast(I32))
             elif what == "s":
                 for r in range(4):

@@ -21,7 +21,7 @@ EPS = 1e-5
 FLOPS = 2 * B * K * N
 
 GROUPS = (2, 2, 4, 4, 4, 2, 2)
-LOADS = (("x", 0, 2), ("v", 0, 0), ("x", 2, 4), ("x", 4, 8), ("w", 0, 0), ("s", 0, 0), ("x", 8, 12), ("y", 0, 4), ("x", 12, 16), ("x", 16, 20), ("y", 4, 8), ("y", 8, 12), ("y", 12, 16), ("y", 16, 20))
+LOADS = (("x", 0, 2), ("v", 0, 0), ("x", 2, 4), ("x", 4, 8), ("w", 0, 0), ("s", 0, 0), ("x", 8, 12), ("x", 12, 16), ("y", 0, 4), ("x", 16, 20), ("y", 4, 8), ("y", 8, 12), ("y", 12, 16), ("y", 16, 20))
 CLS = "abababcabcabcabcaccc"
 AHEAD = 3
 PRE = 4

@@ -22,7 +22,7 @@ FLOPS = 2 * B * K * N
 
 GROUPS = (2, 2, 4, 4, 4, 2, 2)
 LOADS = (("x", 0, 2), ("v", 0, 0), ("x", 2, 4), ("x", 4, 8), ("w", 0, 0), ("s", 0, 0), ("x", 8, 12), ("x", 12, 16), ("y", 0, 4), ("x", 16, 20), ("y", 4, 8), ("y", 8, 12), ("y", 12, 16), ("y", 16, 20))
-CLS = "abababcabcabcabcaccc"
+CLS = "abababababcabcaccccc"
 AHEAD = 3
 PRE = 4
 S2_VECTOR = ((0, 0), (1, 0))

@@ -22,12 +22,10 @@ FLOPS = 2 * B * K * N
 
 GROUPS = (2, 2, 4, 4, 4, 2, 2)
 LOADS = (("x", 0, 2), ("v", 0, 0), ("x", 2, 4), ("x", 4, 8), ("w", 0, 0), ("s", 0, 0), ("x", 8, 12), ("x", 12, 16), ("y", 0, 4), ("x", 16, 20), ("y", 4, 8), ("y", 8, 12), ("y", 12, 16), ("y", 16, 20))
-CLS = "abababababcabcaccccc"
-AHEAD = 3
-PRE = 4
-S2_VECTOR = ((0, 0), (1, 0))
+CLS = "ababababcabcacccccca"
+X_WITH = {1: (3,), 2: (4,), 3: (5, 6)}
+S2_VECTOR = ()
 S5_VECTOR = ((0, 1), (0, 3), (1, 1), (1, 3))
-PINNED = True
 
 
 def tile_modelnew_kernel(
@@ -43,8 +41,7 @@ def tile_modelnew_kernel(
     with ExitStack() as ctx:
         sb = ctx.enter_context(tc.tile_pool(name="sb", bufs=1))
         ps = ctx.enter_context(tc.psum_pool(name="ps", bufs=8))
-        if PINNED:
-            ctx.enter_context(tc.manual_schedule())
+        ctx.enter_context(tc.manual_schedule())
 
         def bank(shape, dtype, name):
             return ps.tile(shape, dtype, name=name, tag="bank")
@@ -125,40 +122,38 @@ def tile_modelnew_kernel(
             codes_of[g] = codes
             plane_of[g] = plane
 
-        s1(0)
-        s2(0)
-        vps = bank([P, P], BF16, "vps")
-        nc.tensor.transpose(vps[:], vt[:], ident_b[:])
-        vv = sb.tile([P, 5 * NCH], F32, name="vv")
-        nc.vector.tensor_copy(out=vv[:], in_=vps[:, 0 : 5 * NCH])
-        c_bias = vv[:, 0:NCH]
-        c_mean = vv[:, NCH : 2 * NCH]
-        c_var = vv[:, 2 * NCH : 3 * NCH]
-        c_nw = vv[:, 3 * NCH : 4 * NCH]
-        c_nb = vv[:, 4 * NCH : 5 * NCH]
-        ve = sb.tile([P, NCH], F32, name="ve")
-        nc.vector.tensor_scalar_add(out=ve[:], in0=c_var, scalar1=EPS)
-        sd = sb.tile([P, NCH], F32, name="sd")
-        nc.scalar.activation(out=sd[:], in_=ve[:], func=ACT.Sqrt)
-        dm = sb.tile([P, NCH], F32, name="dm")
-        nc.vector.tensor_tensor(out=dm[:], in0=c_bias, in1=c_mean, op=ALU.subtract)
-        s3(0)
-        rs = sb.tile([P, NCH], F32, name="rs")
-        nc.vector.reciprocal(out=rs[:], in_=sd[:])
-        a_sc = sb.tile([P, NCH], F32, name="a_sc")
-        nc.vector.tensor_tensor(out=a_sc[:], in0=rs[:], in1=c_nw, op=ALU.mult)
-        da = sb.tile([P, NCH], F32, name="da")
-        nc.vector.tensor_tensor(out=da[:], in0=dm[:], in1=a_sc[:], op=ALU.mult)
-        c_sh = sb.tile([P, NCH], F32, name="c_sh")
-        nc.vector.tensor_tensor(out=c_sh[:], in0=da[:], in1=c_nb, op=ALU.add)
-        for g in range(1, min(AHEAD, n_groups)):
-            s1(g)
-            s2(g)
-            s3(g)
+        sc_of = {}
+
+        def scale_shift_start():
+            vps = bank([P, P], BF16, "vps")
+            nc.tensor.transpose(vps[:], vt[:], ident_b[:])
+            sd = sb.tile([P, NCH], F32, name="sd")
+            nc.scalar.activation(out=sd[:], in_=vps[:, 2 * NCH : 3 * NCH], func=ACT.Sqrt, bias=EPS)
+            vv = sb.tile([P, 5 * NCH], F32, name="vv")
+            nc.vector.tensor_copy(out=vv[:], in_=vps[:, 0 : 5 * NCH])
+            dm = sb.tile([P, NCH], F32, name="dm")
+            nc.vector.tensor_tensor(out=dm[:], in0=vv[:, 0:NCH], in1=vv[:, NCH : 2 * NCH], op=ALU.subtract)
+            dw = sb.tile([P, NCH], F32, name="dw")
+            nc.vector.tensor_tensor(out=dw[:], in0=dm[:], in1=vv[:, 3 * NCH : 4 * NCH], op=ALU.mult)
+            sc_of.update(sd=sd, vv=vv, dw=dw)
+
+        def scale_shift_end():
+            vv = sc_of["vv"]
+            rs = sb.tile([P, NCH], F32, name="rs")
+            nc.vector.reciprocal(out=rs[:], in_=sc_of["sd"][:])
+            da = sb.tile([P, NCH], F32, name="da")
+            nc.vector.tensor_tensor(out=da[:], in0=rs[:], in1=sc_of["dw"][:], op=ALU.mult)
+            a_sc = sb.tile([P, NCH], F32, name="a_sc")
+            nc.vector.tensor_tensor(out=a_sc[:], in0=rs[:], in1=vv[:, 3 * NCH : 4 * NCH], op=ALU.mult)
+            c_sh = sb.tile([P, NCH], F32, name="c_sh")
+            nc.vector.tensor_tensor(out=c_sh[:], in0=da[:], in1=vv[:, 4 * NCH : 5 * NCH], op=ALU.add)
+            sc_of.update(a=a_sc, c=c_sh)
 
         def mx(g):
             r = GROUPS[g]
             zts = []
+            a_sc = sc_of["a"]
+            c_sh = sc_of["c"]
             for c in range(NCH):
                 lin = bank([P, P * r], F32, "lin%d_%d" % (g, c))
                 nc.tensor.matmul_mx(
@@ -231,27 +226,41 @@ def tile_modelnew_kernel(
             elif t % 2 == 1:
                 nc.sync.dma_start(out=ov[:, t - 1 : t + 1, :], in_=pair_of[t][:])
 
-        for g in range(n_groups + 1):
-            if g < n_groups:
+        s1(0)
+        s2(0)
+        scale_shift_start()
+        s1(1)
+        s2(1)
+        s3(0)
+        scale_shift_end()
+        s3(1)
+        s1(2)
+        s2(2)
+        mx(0)
+        mx(1)
+        s3(2)
+        for g in range(1, n_groups + 1):
+            if 2 <= g < n_groups:
                 mx(g)
-            back = list(range(first[g - 1], first[g - 1] + GROUPS[g - 1])) if g >= 1 else []
-            ahead = g + AHEAD if g + AHEAD < n_groups else None
-            for t in back[:PRE]:
+            back = list(range(first[g - 1], first[g - 1] + GROUPS[g - 1]))
+            ahead = X_WITH.get(g, ())
+            for i, t in enumerate(back):
+                if i == (0 if g == 1 else len(back) // 2):
+                    for a in ahead:
+                        s1(a)
+                    if g == 1:
+                        for a in ahead:
+                            s2(a)
                 if CLS[t] == "c":
                     add_y(t)
                 s6(g - 1, t)
-            if ahead is not None:
-                s1(ahead)
-            for t in back[PRE:]:
-                if CLS[t] == "c":
-                    add_y(t)
-                s6(g - 1, t)
-            if ahead is not None:
-                s2(ahead)
+            if g > 1:
+                for a in ahead:
+                    s2(a)
             for t in back:
                 p1(t)
                 if t >= 1:
                     finish(t - 1)
-            if ahead is not None:
-                s3(ahead)
+            for a in ahead:
+                s3(a)
         finish(NT - 1)

@@ -22,9 +22,10 @@ FLOPS = 2 * B * K * N
 
 GROUPS = (2, 2, 4, 4, 4, 2, 2)
 LOADS = (("x", 0, 2), ("v", 0, 0), ("x", 2, 4), ("x", 4, 8), ("w", 0, 0), ("s", 0, 0), ("x", 8, 12), ("x", 12, 16), ("y", 0, 4), ("x", 16, 20), ("y", 4, 8), ("y", 8, 12), ("y", 12, 16), ("y", 16, 20))
-CLS = "ababababcabcacccccca"
+CLS = "abababababcabcaccccc"
 X_WITH = {1: (3,), 2: (4,), 3: (5, 6)}
 S2_VECTOR = ()
+SORTED = (4,)
 S5_VECTOR = ((0, 1), (0, 3), (1, 1), (1, 3))
 
 
@@ -62,6 +63,8 @@ def tile_modelnew_kernel(
 
         w_sb = sb.tile([P, 2 * N], U8, name="w_sb", align_bytes=64)
         x_of = {}
+        chunk_of = {}
+        sorted_of = {}
         y_of = {}
         for what, t0, t1 in LOADS:
             if what == "v":
@@ -78,6 +81,7 @@ def tile_modelnew_kernel(
                 nc.sync.dma_start(out=chunk[:], in_=src[:, t0:t1, :])
                 for t in range(t0, t1):
                     table[t] = chunk[:, t - t0, :]
+                    chunk_of[what, t] = chunk
 
         xt_of = {}
         grouped_of = {}
@@ -88,6 +92,14 @@ def tile_modelnew_kernel(
         res_of = {}
         pair_of = {}
 
+        def s0(g):
+            words = sb.tile([P, GROUPS[g], 2, P], F32, name="words%d" % g)
+            nc.vector.tensor_copy(
+                out=words[:],
+                in_=chunk_of["x", first[g]][:].bitcast(F32).rearrange("p t (w u) -> p t u w", u=2),
+            )
+            sorted_of[g] = words
+
         def s1(g):
             r = GROUPS[g]
             tiles = []
@@ -97,7 +109,8 @@ def tile_modelnew_kernel(
                 for jj in range(cnt):
                     xw = x_of[first[g] + b0 + jj].bitcast(F32)
                     for u in range(2):
-                        nc.tensor.transpose(xt[:, u, P * jj : P * (jj + 1)], xw[:, u : K // 2 : 2], ident_f[:])
+                        words = sorted_of[g][:, b0 + jj, u, :] if g in SORTED else xw[:, u : K // 2 : 2]
+                        nc.tensor.transpose(xt[:, u, P * jj : P * (jj + 1)], words, ident_f[:])
                 tiles.append((b0, cnt, xt))
             xt_of[g] = tiles
 
@@ -239,6 +252,8 @@ def tile_modelnew_kernel(
         mx(0)
         mx(1)
         s3(2)
+        for g in SORTED:
+            s0(g)
         for g in range(1, n_groups + 1):
             if 2 <= g < n_groups:
                 mx(g)

@@ -22,11 +22,11 @@ FLOPS = 2 * B * K * N
 
 GROUPS = (2, 2, 4, 4, 4, 2, 2)
 LOADS = (("x", 0, 2), ("v", 0, 0), ("x", 2, 4), ("x", 4, 8), ("w", 0, 0), ("s", 0, 0), ("x", 8, 12), ("x", 12, 16), ("y", 0, 4), ("x", 16, 20), ("y", 4, 8), ("y", 8, 12), ("y", 12, 16), ("y", 16, 20))
-CLS = "abababababcabcaccccc"
+CLS = "ababababcabcacaccccc"
 X_WITH = {1: (3,), 2: (4,), 3: (5, 6)}
 S2_VECTOR = ()
 SORTED = (4,)
-S5_VECTOR = ((0, 1), (0, 3), (1, 1), (1, 3))
+S5_VECTOR = ((0, 2), (0, 3), (1, 2), (1, 3))
 
 
 def tile_modelnew_kernel(
@@ -167,10 +167,14 @@ def tile_modelnew_kernel(
             zts = []
             a_sc = sc_of["a"]
             c_sh = sc_of["c"]
+            lins = []
             for c in range(NCH):
-                lin = bank([P, P * r], F32, "lin%d_%d" % (g, c))
+                if c % (4 // r) == 0:
+                    pair = bank([P, 4 // r, P * r], F32, "lin%d_%d" % (g, c))
+                lin = pair[:, c % (4 // r), :]
+                lins.append(lin)
                 nc.tensor.matmul_mx(
-                    out=lin[:],
+                    out=lin,
                     lhsT=w_sb[:, 2 * P * c : 2 * P * (c + 1)].bitcast(FP4X4),
                     lhsT_scale=w_pl[:, P * c : P * (c + 1)],
                     rhs=codes_of[g][:].bitcast(FP8X4),
@@ -178,11 +182,13 @@ def tile_modelnew_kernel(
                     start=True,
                     stop=True,
                 )
+            for c in range(NCH):
+                lin = lins[c]
                 zt = sb.tile([P, P * r], F32, name="zt%d_%d" % (g, c))
                 if (g, c) in S5_VECTOR:
                     nc.vector.tensor_scalar(
                         out=zt[:],
-                        in0=lin[:],
+                        in0=lin,
                         scalar1=a_sc[:, c : c + 1],
                         scalar2=c_sh[:, c : c + 1],
                         op0=ALU.mult,
@@ -190,7 +196,7 @@ def tile_modelnew_kernel(
                     )
                 else:
                     nc.scalar.activation(
-                        out=zt[:], in_=lin[:], func=ACT.Identity, bias=c_sh[:, c : c + 1], scale=a_sc[:, c : c + 1]
+                        out=zt[:], in_=lin, func=ACT.Identity, bias=c_sh[:, c : c + 1], scale=a_sc[:, c : c + 1]
                     )
                 zts.append(zt)
             zt_of[g] = zts

from contextlib import ExitStack

import concourse.mybir as mybir
from concourse.masks import make_identity

F32 = mybir.dt.float32
BF16 = mybir.dt.bfloat16
I32 = mybir.dt.int32
U32 = mybir.dt.uint32
U8 = mybir.dt.uint8
FP8X4 = mybir.dt.float8_e4m3fn_x4
FP4X4 = mybir.dt.float4_e2m1fn_x4
ACT = mybir.ActivationFunctionType
ALU = mybir.AluOpType

P = 128
B, K, N = 2560, 512, 512
NT = B // P
NCH = N // P
EPS = 1e-5
FLOPS = 2 * B * K * N

GROUPS = (2, 2, 4, 4, 4, 2, 2)
LOADS = (("x", 0, 2), ("v", 0, 0), ("x", 2, 4), ("x", 4, 8), ("w", 0, 0), ("s", 0, 0), ("x", 8, 12), ("x", 12, 16), ("y", 0, 4), ("x", 16, 20), ("y", 4, 8), ("y", 8, 12), ("y", 12, 16), ("y", 16, 20))
CLS = "ababababcabcacaccccc"
X_WITH = {1: (3,), 2: (4,), 3: (5, 6)}
S2_VECTOR = ()
SORTED = (4,)
S5_VECTOR = ((0, 2), (0, 3), (1, 2), (1, 3))


def tile_modelnew_kernel(
    tc, x, y, weight_words, weight_scales, bias, running_mean, running_var, norm_weight, norm_bias, out
):
    nc = tc.nc
    xv = x.rearrange("(p t) k -> p t k", t=NT)
    yv = y.rearrange("(p t) n -> p t n", t=NT)
    ov = out.rearrange("(p t) n -> p t n", t=NT)
    n_groups = len(GROUPS)
    first = [sum(GROUPS[:g]) for g in range(n_groups)]

    with ExitStack() as ctx:
        sb = ctx.enter_context(tc.tile_pool(name="sb", bufs=1))
        ps = ctx.enter_context(tc.psum_pool(name="ps", bufs=8))
        ctx.enter_context(tc.manual_schedule())

        def bank(shape, dtype, name):
            return ps.tile(shape, dtype, name=name, tag="bank")

        vt = sb.tile([P, P], BF16, name="vt")
        nc.gpsimd.memset(vt[:], 0.0)
        w_pl = sb.tile([P, N], U8, name="w_pl", align_bytes=64)
        nc.vector.memset(w_pl[:].bitcast(I32), 0)
        one = sb.tile([P, 1], F32, name="one")
        nc.vector.memset(one[:], 1.0)
        warm = sb.tile([P, 1], F32, name="warm")
        nc.scalar.activation(out=warm[:], in_=one[:], func=ACT.Sqrt)

        ident_f = sb.tile([P, P], F32, name="ident_f")
        make_identity(nc, ident_f[:])
        ident_b = sb.tile([P, P], BF16, name="ident_b")
        make_identity(nc, ident_b[:])

        w_sb = sb.tile([P, 2 * N], U8, name="w_sb", align_bytes=64)
        x_of = {}
        chunk_of = {}
        sorted_of = {}
        y_of = {}
        for what, t0, t1 in LOADS:
            if what == "v":
                for v, vec in enumerate((bias, running_mean, running_var, norm_weight, norm_bias)):
                    nc.sync.dma_start(out=vt[NCH * v : NCH * (v + 1), :], in_=vec.rearrange("(c p) -> c p", p=P))
            elif what == "w":
                nc.sync.dma_start(out=w_sb[:].bitcast(I32), in_=weight_words[0].bitcast(I32))
            elif what == "s":
                for r in range(4):
                    nc.sync.dma_start(out=w_pl[r:P:32, :].bitcast(I32), in_=weight_scales[0, r:16:4, :].bitcast(I32))
            else:
                src, table = (xv, x_of) if what == "x" else (yv, y_of)
                chunk = sb.tile([P, t1 - t0, K], BF16, name="%s%d" % (what, t0))
                nc.sync.dma_start(out=chunk[:], in_=src[:, t0:t1, :])
                for t in range(t0, t1):
                    table[t] = chunk[:, t - t0, :]
                    chunk_of[what, t] = chunk

        xt_of = {}
        grouped_of = {}
        codes_of = {}
        plane_of = {}
        zt_of = {}
        zb_of = {}
        res_of = {}
        pair_of = {}

        def s0(g):
            words = sb.tile([P, GROUPS[g], 2, P], F32, name="words%d" % g)
            nc.vector.tensor_copy(
                out=words[:],
                in_=chunk_of["x", first[g]][:].bitcast(F32).rearrange("p t (w u) -> p t u w", u=2),
            )
            sorted_of[g] = words

        def s1(g):
            r = GROUPS[g]
            tiles = []
            for b0 in range(0, r, 2):
                cnt = min(2, r - b0)
                xt = bank([P, 2, P * cnt], F32, "xt%d_%d" % (g, b0))
                for jj in range(cnt):
                    xw = x_of[first[g] + b0 + jj].bitcast(F32)
                    for u in range(2):
                        words = sorted_of[g][:, b0 + jj, u, :] if g in SORTED else xw[:, u : K // 2 : 2]
                        nc.tensor.transpose(xt[:, u, P * jj : P * (jj + 1)], words, ident_f[:])
                tiles.append((b0, cnt, xt))
            xt_of[g] = tiles

        def s2(g):
            r = GROUPS[g]
            grouped = sb.tile([P, 4 * P * r], BF16, name="grp%d" % g, align_bytes=64)
            gv = grouped[:].bitcast(F32).rearrange("p (r u) -> p r u", u=2)
            for b0, cnt, xt in xt_of[g]:
                dst = gv[:, P * b0 : P * (b0 + cnt), :]
                src = xt[:].rearrange("p u r -> p r u")
                if (g, b0) in S2_VECTOR:
                    nc.vector.tensor_copy(out=dst, in_=src)
                else:
                    nc.scalar.copy(out=dst, in_=src)
            grouped_of[g] = grouped

        def s3(g):
            r = GROUPS[g]
            codes = sb.tile([P, P * r], U32, name="codes%d" % g, align_bytes=64)
            plane = sb.tile([P, P * r], U8, name="plane%d" % g, align_bytes=64)
            nc.vector.quantize_mx(out=codes[:].bitcast(FP8X4), scales=plane[:], in_=grouped_of[g][:])
            codes_of[g] = codes
            plane_of[g] = plane

        sc_of = {}

        def scale_shift_start():
            vps = bank([P, P], BF16, "vps")
            nc.tensor.transpose(vps[:], vt[:], ident_b[:])
            sd = sb.tile([P, NCH], F32, name="sd")
            nc.scalar.activation(out=sd[:], in_=vps[:, 2 * NCH : 3 * NCH], func=ACT.Sqrt, bias=EPS)
            vv = sb.tile([P, 5 * NCH], F32, name="vv")
            nc.vector.tensor_copy(out=vv[:], in_=vps[:, 0 : 5 * NCH])
            dm = sb.tile([P, NCH], F32, name="dm")
            nc.vector.tensor_tensor(out=dm[:], in0=vv[:, 0:NCH], in1=vv[:, NCH : 2 * NCH], op=ALU.subtract)
            dw = sb.tile([P, NCH], F32, name="dw")
            nc.vector.tensor_tensor(out=dw[:], in0=dm[:], in1=vv[:, 3 * NCH : 4 * NCH], op=ALU.mult)
            sc_of.update(sd=sd, vv=vv, dw=dw)

        def scale_shift_end():
            vv = sc_of["vv"]
            rs = sb.tile([P, NCH], F32, name="rs")
            nc.vector.reciprocal(out=rs[:], in_=sc_of["sd"][:])
            da = sb.tile([P, NCH], F32, name="da")
            nc.vector.tensor_tensor(out=da[:], in0=rs[:], in1=sc_of["dw"][:], op=ALU.mult)
            a_sc = sb.tile([P, NCH], F32, name="a_sc")
            nc.vector.tensor_tensor(out=a_sc[:], in0=rs[:], in1=vv[:, 3 * NCH : 4 * NCH], op=ALU.mult)
            c_sh = sb.tile([P, NCH], F32, name="c_sh")
            nc.vector.tensor_tensor(out=c_sh[:], in0=da[:], in1=vv[:, 4 * NCH : 5 * NCH], op=ALU.add)
            sc_of.update(a=a_sc, c=c_sh)

        def mx(g):
            r = GROUPS[g]
            zts = []
            a_sc = sc_of["a"]
            c_sh = sc_of["c"]
            lins = []
            for c in range(NCH):
                if c % (4 // r) == 0:
                    pair = bank([P, 4 // r, P * r], F32, "lin%d_%d" % (g, c))
                lin = pair[:, c % (4 // r), :]
                lins.append(lin)
                nc.tensor.matmul_mx(
                    out=lin,
                    lhsT=w_sb[:, 2 * P * c : 2 * P * (c + 1)].bitcast(FP4X4),
                    lhsT_scale=w_pl[:, P * c : P * (c + 1)],
                    rhs=codes_of[g][:].bitcast(FP8X4),
                    rhs_scale=plane_of[g][:],
                    start=True,
                    stop=True,
                )
            for c in range(NCH):
                lin = lins[c]
                zt = sb.tile([P, P * r], F32, name="zt%d_%d" % (g, c))
                if (g, c) in S5_VECTOR:
                    nc.vector.tensor_scalar(
                        out=zt[:],
                        in0=lin,
                        scalar1=a_sc[:, c : c + 1],
                        scalar2=c_sh[:, c : c + 1],
                        op0=ALU.mult,
                        op1=ALU.add,
                    )
                else:
                    nc.scalar.activation(
                        out=zt[:], in_=lin, func=ACT.Identity, bias=c_sh[:, c : c + 1], scale=a_sc[:, c : c + 1]
                    )
                zts.append(zt)
            zt_of[g] = zts

        def s6(g, t):
            j = t - first[g]
            if CLS[t] == "c":
                zb = zb_of[t]
            else:
                zb = bank([P, N], F32, "zb%d" % t)
            for c in range(NCH):
                if CLS[t] == "c":
                    nc.tensor.matmul(
                        out=zb[:, P * c : P * (c + 1)],
                        lhsT=zt_of[g][c][:, P * j : P * (j + 1)],
                        rhs=ident_f[:],
                        is_transpose=True,
                        start=False,
                        stop=(c == NCH - 1),
                    )
                else:
                    nc.tensor.transpose(zb[:, P * c : P * (c + 1)], zt_of[g][c][:, P * j : P * (j + 1)], ident_f[:])
            zb_of[t] = zb

        def add_y(t):
            zb = bank([P, N], F32, "zb%d" % t)
            nc.tensor.matmul(out=zb[:], lhsT=ident_b[:], rhs=y_of[t], start=True, stop=False)
            zb_of[t] = zb

        def p1(t):
            if t % 2 == 0:
                pair = sb.tile([P, 2, N], F32, name="res%d" % t)
                pair_of[t] = pair
                pair_of[t + 1] = pair
            res_of[t] = pair_of[t][:, t % 2, :]
            nc.vector.tensor_tensor(out=res_of[t], in0=zb_of[t][:], in1=y_of[t], op=ALU.mult if CLS[t] == "c" else ALU.add)

        def finish(t):
            res = res_of[t]
            if CLS[t] == "b":
                nc.gpsimd.tensor_tensor(out=res, in0=res, in1=y_of[t], op=ALU.mult)
            elif CLS[t] == "a":
                nc.vector.tensor_tensor(out=res, in0=res, in1=y_of[t], op=ALU.mult)
            if t >= NT - 2:
                nc.sync.dma_start(out=ov[:, t, :], in_=res)
            elif t % 2 == 1:
                nc.sync.dma_start(out=ov[:, t - 1 : t + 1, :], in_=pair_of[t][:])

        s1(0)
        s2(0)
        scale_shift_start()
        s1(1)
        s2(1)
        s3(0)
        scale_shift_end()
        s3(1)
        s1(2)
        s2(2)
        mx(0)
        mx(1)
        s3(2)
        for g in SORTED:
            s0(g)
        for g in range(1, n_groups + 1):
            if 2 <= g < n_groups:
                mx(g)
            back = list(range(first[g - 1], first[g - 1] + GROUPS[g - 1]))
            ahead = X_WITH.get(g, ())
            for i, t in enumerate(back):
                if i == (0 if g == 1 else len(back) // 2):
                    for a in ahead:
                        s1(a)
                    if g == 1:
                        for a in ahead:
                            s2(a)
                if CLS[t] == "c":
                    add_y(t)
                s6(g - 1, t)
            if g > 1:
                for a in ahead:
                    s2(a)
            for t in back:
                p1(t)
                if t >= 1:
                    finish(t - 1)
            for a in ahead:
                s3(a)
        finish(NT - 1)
